import numpy as np
import ml_dtypes


BF16 = ml_dtypes.bfloat16


def bf(x):
    return np.asarray(x, np.float32).astype(BF16)


def f64(x):
    return np.asarray(x).astype(np.float64)


E2M1 = np.array([0.0, 0.5, 1.0, 1.5, 2.0, 3.0, 4.0, 6.0, -0.0, -0.5, -1.0, -1.5, -2.0, -3.0, -4.0, -6.0])


def pack_weight(w, fmt):
    k, n = w.shape
    w = f64(bf(w)).reshape(k // 32, 32, n)
    amax = np.abs(w).max(1)
    if fmt == "e4m3":
        byte = np.frexp(amax)[1] - 1 + 127 - 7
    else:
        mant, ex = np.frexp(amax / 6.0)
        byte = np.where(mant > 0.5, ex, ex - 1) + 127
    byte = np.clip(np.where(amax > 0, byte, 1), 1, 254)
    scaled = (w * np.exp2(127.0 - byte)[:, None, :]).reshape(k, n).astype(np.float32)
    by_word = np.ascontiguousarray(scaled.reshape(k // 512, 128, 4, n).transpose(0, 1, 3, 2))
    if fmt == "e4m3":
        words = by_word.astype(ml_dtypes.float8_e4m3fn).view(np.uint8)
    else:
        c = by_word.astype(ml_dtypes.float4_e2m1fn).view(np.uint8) & 0xF
        words = c[..., 0::2] | (c[..., 1::2] << 4)
    return np.ascontiguousarray(words), np.ascontiguousarray(byte.astype(np.uint8).reshape(k // 512, 16, n))


def unpack_weight(words, scales, fmt):
    g, p, n, _ = words.shape
    if fmt == "e4m3":
        vals = np.ascontiguousarray(words).view(ml_dtypes.float8_e4m3fn).astype(np.float64)
    else:
        nib = np.empty((g, p, n, 4), np.uint8)
        nib[..., 0::2] = words & 0xF
        nib[..., 1::2] = words >> 4
        vals = E2M1[nib]
    vals = vals * np.repeat(np.exp2(scales.astype(np.float64) - 127.0), 8, axis=1)[..., None]
    return vals.transpose(0, 1, 3, 2).reshape(g * 512, n)

def pack4(w):
    words, scales = pack_weight(w, "e2m1")
    return words.reshape(words.shape[0], 128, -1), scales


def unpack4(words, scales):
    return unpack_weight(words.reshape(words.shape[0], 128, -1, 2), scales, "e2m1")


def kspread(k):
    return np.exp2(np.repeat(np.random.randint(-6, 7, k // 32), 32).astype(np.float64))


B, S, DIM, H, NOPE, ROPE_D, VD = 2, 64, 4096, 16, 128, 64, 128
QKD = NOPE + ROPE_D
BASE = 10000.0


def rope_cos_sin(seq_len):
    theta = 1.0 / BASE ** (f64(np.arange(0, ROPE_D, 2)) / ROPE_D)
    pos = f64(np.arange(seq_len))
    ang = pos[:, None] * theta[None, :]
    return np.cos(ang), np.sin(ang)


def apply_rope(v, cos, sin):
    b, s, h, d = v.shape
    vs = v.reshape(b, s, h, d // 2, 2)
    c = cos[None, :, None, :]
    sn = sin[None, :, None, :]
    out = np.stack([vs[..., 0] * c - vs[..., 1] * sn, vs[..., 1] * c + vs[..., 0] * sn], axis=-1)
    return out.reshape(b, s, h, d)


def setup_inputs():
    s = kspread(DIM)
    x = np.random.standard_normal((B, S, DIM)) * s
    x_words, x_scales = pack4(np.ascontiguousarray(x.reshape(B * S, DIM).T))
    Wq_words, Wq_scales = pack4(np.random.standard_normal((DIM, H * QKD)) / np.sqrt(DIM) / s[:, None])
    Wk_words, Wk_scales = pack4(np.random.standard_normal((DIM, H * QKD)) / np.sqrt(DIM) / s[:, None])
    return {'x_words': x_words, 'x_scales': x_scales,
            'Wq_words': Wq_words, 'Wq_scales': Wq_scales,
            'Wk_words': Wk_words, 'Wk_scales': Wk_scales}


def reference(x_words, x_scales, Wq_words, Wq_scales, Wk_words, Wk_scales):
    xq = unpack4(x_words, x_scales).T.reshape(B, S, DIM)
    q = (xq @ unpack4(Wq_words, Wq_scales)).reshape(B, S, H, QKD)
    k = (xq @ unpack4(Wk_words, Wk_scales)).reshape(B, S, H, QKD)
    cos, sin = rope_cos_sin(S)
    q = np.concatenate([q[..., :NOPE], apply_rope(q[..., NOPE:], cos, sin)], axis=-1)
    k = np.concatenate([k[..., :NOPE], apply_rope(k[..., NOPE:], cos, sin)], axis=-1)
    return q, k

@@ -1,0 +1,180 @@
+from contextlib import ExitStack
+
+import concourse.mybir as mybir
+
+F32 = mybir.dt.float32
+I32 = mybir.dt.int32
+U8 = mybir.dt.uint8
+FP4X4 = mybir.dt.float4_e2m1fn_x4
+ALU = mybir.AluOpType
+ACTF = mybir.ActivationFunctionType
+
+P = 128
+PASSES = 8
+COLS = 3072
+N_TILE = 512
+TILES = COLS // N_TILE
+RUN = 4
+BLOCK = 64
+PAIRS = 32
+TWO_PI = 6.283185307179586
+ROPE_BASE = 10000.0
+
+FLOPS = 2 * 128 * 4096 * 6144
+
+
+def tile_mla_pa_kernel(tc, x_words, x_scales, Wq_words, Wq_scales, Wk_words, Wk_scales, out_0, out_1):
+    nc = tc.nc
+    w_words = [Wq_words, Wk_words]
+    w_scales = [Wq_scales, Wk_scales]
+    out_rows = [o.rearrange("b s h d -> (b s) (h d)") for o in (out_0, out_1)]
+
+    with ExitStack() as ctx:
+        keep = ctx.enter_context(tc.tile_pool(name="keep", bufs=1))
+        work = ctx.enter_context(tc.tile_pool(name="work", bufs=4))
+        psum = ctx.enter_context(tc.psum_pool(name="psum", bufs=8))
+        ctx.enter_context(tc.manual_schedule())
+
+        xw = keep.tile([P, PASSES, 256], U8, name="xw", align_bytes=64)
+        xs = keep.tile([P, PASSES, P], U8, name="xs", align_bytes=64)
+        codes = [[keep.tile([P, 2 * COLS], U8, name="w%d_%d" % (t, g), align_bytes=64) for g in range(PASSES)] for t in range(2)]
+        planes = [[keep.tile([P, RUN, COLS], U8, name="s%d_%d" % (t, r), align_bytes=64) for r in range(PASSES // RUN)] for t in range(2)]
+        res = [keep.tile([P, COLS], F32, name="res%d" % t) for t in range(2)]
+
+        def zero(plane):
+            nc.vector.memset(plane.bitcast(I32), 0)
+
+        def load_codes(t, g):
+            nc.sync.dma_start(out=codes[t][g][:].bitcast(I32), in_=w_words[t][g].bitcast(I32))
+
+        def load_scale_rows(plane, rows):
+            for r in range(4):
+                nc.sync.dma_start(
+                    out=plane[r:P:32, :, :].bitcast(I32),
+                    in_=rows[:, r:16:4, :].rearrange("g q n -> q g n").bitcast(I32),
+                )
+
+        def load_scales(t, run):
+            load_scale_rows(planes[t][run], w_scales[t][run * RUN : (run + 1) * RUN])
+
+        def multiply(t, g, accs):
+            for j in range(TILES):
+                nc.tensor.matmul_mx(
+                    out=accs[j][:],
+                    lhsT=xw[:, g, :].bitcast(FP4X4),
+                    lhsT_scale=xs[:, g, :],
+                    rhs=codes[t][g][:, 2 * N_TILE * j : 2 * N_TILE * (j + 1)].bitcast(FP4X4),
+                    rhs_scale=planes[t][g // RUN][:, g % RUN, N_TILE * j : N_TILE * (j + 1)],
+                    start=(g == 0),
+                    stop=(g == PASSES - 1),
+                )
+
+        zero(xs[:].rearrange("p g n -> p (g n)"))
+        zero(planes[0][0][:].rearrange("p g n -> p (g n)"))
+        nc.sync.dma_start(out=xw[:].bitcast(I32), in_=x_words.rearrange("g p n -> p g n").bitcast(I32))
+        load_codes(0, 0)
+        load_codes(0, 1)
+        load_scale_rows(xs, x_scales)
+        load_scales(0, 0)
+        for g in range(2, 6):
+            load_codes(0, g)
+
+        pos_i = keep.tile([P, 1], I32, name="pos_i")
+        nc.gpsimd.iota(pos_i[0:64, :], pattern=[[0, 1]], base=0, channel_multiplier=1)
+        nc.gpsimd.iota(pos_i[64:128, :], pattern=[[0, 1]], base=0, channel_multiplier=1)
+        pos = keep.tile([P, 1], F32, name="pos")
+        nc.vector.tensor_copy(out=pos[:], in_=pos_i[:])
+        theta = keep.tile([P, PAIRS], F32, name="theta")
+        nc.vector.memset(theta[:, 0:1], 1.0)
+        width = 1
+        while width < PAIRS:
+            nc.vector.tensor_scalar_mul(out=theta[:, width : 2 * width], in0=theta[:, 0:width], scalar1=ROPE_BASE ** (-2.0 * width / BLOCK))
+            width *= 2
+        turns = keep.tile([P, PAIRS], F32, name="turns")
+        nc.vector.tensor_scalar(out=turns[:], in0=theta[:], scalar1=pos[:, 0:1], scalar2=1.0 / TWO_PI, op0=ALU.mult, op1=ALU.mult)
+        phase = keep.tile([P, 2, PAIRS, 2], F32, name="phase")
+        for a, t, shift in ((0, 0, 0.25), (0, 1, 0.25), (1, 0, 0.5), (1, 1, 0.0)):
+            nc.vector.tensor_scalar_add(out=phase[:, a, :, t], in0=turns[:], scalar1=shift)
+        flat = phase[:].rearrange("p a i t -> p (a i t)")
+        whole_i = keep.tile([P, 2 * BLOCK], I32, name="whole_i")
+        nc.vector.tensor_copy(out=whole_i[:], in_=flat)
+        whole = keep.tile([P, 2 * BLOCK], F32, name="whole")
+        nc.vector.tensor_copy(out=whole[:], in_=whole_i[:])
+        frac = keep.tile([P, 2 * BLOCK], F32, name="frac")
+        nc.vector.tensor_sub(out=frac[:], in0=flat, in1=whole[:])
+        minus = keep.tile([P, 2 * BLOCK], F32, name="minus")
+        nc.vector.scalar_tensor_tensor(out=minus[:], in0=frac[:], scalar=0.5, in1=frac[:], op0=ALU.is_gt, op1=ALU.subtract)
+        table = keep.tile([P, 2, 3, BLOCK], F32, name="table")
+        for h in range(3):
+            nc.scalar.activation(out=table[:, :, h, :], in_=minus[:].rearrange("p (a c) -> p a c", a=2), func=ACTF.Sin, scale=-TWO_PI)
+
+        for t, run in ((0, 1), (1, 0), (1, 1)):
+            zero(planes[t][run][:].rearrange("p g n -> p (g n)"))
+
+        load_scales(0, 1)
+        load_codes(0, 6)
+        load_codes(0, 7)
+        load_scales(1, 0)
+        for g in range(0, 4):
+            load_codes(1, g)
+        load_scales(1, 1)
+        load_codes(1, 4)
+        load_codes(1, 5)
+
+        def rotate_products(t, j, acc):
+            first = (2 - 8 * j) % 3
+            count = len(range(first, 8, 3))
+            dst = res[t][:, N_TILE * j : N_TILE * (j + 1)].rearrange("p (b c) -> p b c", c=BLOCK)[:, first:8:3, :]
+            nc.vector.tensor_tensor(
+                out=dst,
+                in0=acc[:].rearrange("p (b c) -> p b c", c=BLOCK)[:, first:8:3, :],
+                in1=table[:, 0, 0:count, :],
+                op=ALU.mult,
+            )
+            cross = work.tile([P, 3, BLOCK], F32, name="cross", tag="cross")
+            nc.vector.tensor_tensor(
+                out=cross[:, 0:count, :].rearrange("p b (i t) -> p b i t", t=2),
+                in0=acc[:].rearrange("p (b i t) -> p b i t", i=PAIRS, t=2)[:, first:8:3, :, ::-1],
+                in1=table[:, 1, 0:count, :].rearrange("p b (i t) -> p b i t", t=2),
+                op=ALU.mult,
+            )
+            return dst, cross[:, 0:count, :]
+
+        def copy_plain(t, j, acc):
+            first = (2 - 8 * j) % 3
+            for c in range(3):
+                if c != first:
+                    nc.scalar.copy(
+                        out=res[t][:, N_TILE * j : N_TILE * (j + 1)].rearrange("p (b c) -> p b c", c=BLOCK)[:, c:8:3, :],
+                        in_=acc[:].rearrange("p (b c) -> p b c", c=BLOCK)[:, c:8:3, :],
+                    )
+
+        def finish(t, accs, after):
+            pending = None
+            for j in range(TILES + 1):
+                if j < TILES:
+                    halves = rotate_products(t, j, accs[j])
+                    copy_plain(t, j, accs[j])
+                if pending is not None:
+                    nc.vector.tensor_add(out=pending[0], in0=pending[0], in1=pending[1])
+                    after(j - 1)
+                pending = halves
+
+        def store(t, lo, hi):
+            nc.sync.dma_start(out=out_rows[t][:, lo:hi], in_=res[t][:, lo:hi])
+
+        accs = [psum.tile([P, N_TILE], F32, name="accq%d" % j, tag="acc") for j in range(TILES)]
+        for g in range(PASSES):
+            multiply(0, g, accs)
+        finish(0, accs, lambda j: None)
+
+        store(0, 0, 1024)
+        load_codes(1, 6)
+        store(0, 1024, 2048)
+        load_codes(1, 7)
+        store(0, 2048, 3072)
+
+        accs = [psum.tile([P, N_TILE], F32, name="acck%d" % j, tag="acc") for j in range(TILES)]
+        for g in range(PASSES):
+            multiply(1, g, accs)
+        finish(1, accs, lambda j: store(1, N_TILE * j, N_TILE * (j + 1)))

@@ -14,7 +14,6 @@ PASSES = 8
 COLS = 3072
 N_TILE = 512
 TILES = COLS // N_TILE
-RUN = 4
 BLOCK = 64
 PAIRS = 32
 TWO_PI = 6.283185307179586
@@ -38,7 +37,7 @@ def tile_mla_pa_kernel(tc, x_words, x_scales, Wq_words, Wq_scales, Wk_words, Wk_
         xw = keep.tile([P, PASSES, 256], U8, name="xw", align_bytes=64)
         xs = keep.tile([P, PASSES, P], U8, name="xs", align_bytes=64)
         codes = [[keep.tile([P, 2 * COLS], U8, name="w%d_%d" % (t, g), align_bytes=64) for g in range(PASSES)] for t in range(2)]
-        planes = [[keep.tile([P, RUN, COLS], U8, name="s%d_%d" % (t, r), align_bytes=64) for r in range(PASSES // RUN)] for t in range(2)]
+        planes = [keep.tile([P, PASSES, COLS], U8, name="s%d" % t, align_bytes=64) for t in range(2)]
         res = [keep.tile([P, COLS], F32, name="res%d" % t) for t in range(2)]
 
         def zero(plane):
@@ -54,8 +53,13 @@ def tile_mla_pa_kernel(tc, x_words, x_scales, Wq_words, Wq_scales, Wk_words, Wk_
                     in_=rows[:, r:16:4, :].rearrange("g q n -> q g n").bitcast(I32),
                 )
 
-        def load_scales(t, run):
-            load_scale_rows(planes[t][run], w_scales[t][run * RUN : (run + 1) * RUN])
+        def load_scales(t):
+            for p in (0, 1, 2, 3, 32, 33, 34, 35):
+                q = 4 * (p // 32) + p % 32
+                nc.sync.dma_start(
+                    out=planes[t][p:P:64, :, :].bitcast(I32),
+                    in_=w_scales[t][:, q:16:8, :].rearrange("g q n -> q g n").bitcast(I32),
+                )
 
         def multiply(t, g, accs):
             for j in range(TILES):
@@ -64,19 +68,19 @@ def tile_mla_pa_kernel(tc, x_words, x_scales, Wq_words, Wq_scales, Wk_words, Wk_
                     lhsT=xw[:, g, :].bitcast(FP4X4),
                     lhsT_scale=xs[:, g, :],
                     rhs=codes[t][g][:, 2 * N_TILE * j : 2 * N_TILE * (j + 1)].bitcast(FP4X4),
-                    rhs_scale=planes[t][g // RUN][:, g % RUN, N_TILE * j : N_TILE * (j + 1)],
+                    rhs_scale=planes[t][:, g, N_TILE * j : N_TILE * (j + 1)],
                     start=(g == 0),
                     stop=(g == PASSES - 1),
                 )
 
         zero(xs[:].rearrange("p g n -> p (g n)"))
-        zero(planes[0][0][:].rearrange("p g n -> p (g n)"))
+        zero(planes[0][:].rearrange("p g n -> p (g n)"))
         nc.sync.dma_start(out=xw[:].bitcast(I32), in_=x_words.rearrange("g p n -> p g n").bitcast(I32))
         load_codes(0, 0)
         load_codes(0, 1)
         load_scale_rows(xs, x_scales)
-        load_scales(0, 0)
-        for g in range(2, 6):
+        load_scales(0)
+        for g in range(2, PASSES):
             load_codes(0, g)
 
         pos_i = keep.tile([P, 1], I32, name="pos_i")
@@ -108,18 +112,10 @@ def tile_mla_pa_kernel(tc, x_words, x_scales, Wq_words, Wq_scales, Wk_words, Wk_
         for h in range(3):
             nc.scalar.activation(out=table[:, :, h, :], in_=minus[:].rearrange("p (a c) -> p a c", a=2), func=ACTF.Sin, scale=-TWO_PI)
 
-        for t, run in ((0, 1), (1, 0), (1, 1)):
-            zero(planes[t][run][:].rearrange("p g n -> p (g n)"))
-
-        load_scales(0, 1)
-        load_codes(0, 6)
-        load_codes(0, 7)
-        load_scales(1, 0)
-        for g in range(0, 4):
+        zero(planes[1][:].rearrange("p g n -> p (g n)"))
+        load_scales(1)
+        for g in range(PASSES):
             load_codes(1, g)
-        load_scales(1, 1)
-        load_codes(1, 4)
-        load_codes(1, 5)
 
         def rotate_products(t, j, acc):
             first = (2 - 8 * j) % 3
@@ -169,9 +165,7 @@ def tile_mla_pa_kernel(tc, x_words, x_scales, Wq_words, Wq_scales, Wk_words, Wk_
         finish(0, accs, lambda j: None)
 
         store(0, 0, 1024)
-        load_codes(1, 6)
         store(0, 1024, 2048)
-        load_codes(1, 7)
         store(0, 2048, 3072)
 
         accs = [psum.tile([P, N_TILE], F32, name="acck%d" % j, tag="acc") for j in range(TILES)]

@@ -14,6 +14,8 @@ PASSES = 8
 COLS = 3072
 N_TILE = 512
 TILES = COLS // N_TILE
+RUN = 4
+PAIR = 2
 BLOCK = 64
 PAIRS = 32
 TWO_PI = 6.283185307179586
@@ -36,15 +38,25 @@ def tile_mla_pa_kernel(tc, x_words, x_scales, Wq_words, Wq_scales, Wk_words, Wk_
 
         xw = keep.tile([P, PASSES, 256], U8, name="xw", align_bytes=64)
         xs = keep.tile([P, PASSES, P], U8, name="xs", align_bytes=64)
-        codes = [[keep.tile([P, 2 * COLS], U8, name="w%d_%d" % (t, g), align_bytes=64) for g in range(PASSES)] for t in range(2)]
-        planes = [keep.tile([P, PASSES, COLS], U8, name="s%d" % t, align_bytes=64) for t in range(2)]
+        codes = [[keep.tile([P, PAIR, 2 * COLS], U8, name="w%d_%d" % (t, h), align_bytes=64) for h in range(PASSES // PAIR - t)] for t in range(2)]
+        tail = [keep.tile([P, PAIR, 4 * N_TILE], U8, name="tail%d" % c, align_bytes=64) for c in range(TILES // 2)]
+        planes = [[keep.tile([P, RUN, COLS], U8, name="s%d_%d" % (t, r), align_bytes=64) for r in range(PASSES // RUN)] for t in range(2)]
         res = [keep.tile([P, COLS], F32, name="res%d" % t) for t in range(2)]
 
         def zero(plane):
             nc.vector.memset(plane.bitcast(I32), 0)
 
-        def load_codes(t, g):
-            nc.sync.dma_start(out=codes[t][g][:].bitcast(I32), in_=w_words[t][g].bitcast(I32))
+        def load_codes(t, h):
+            nc.sync.dma_start(
+                out=codes[t][h][:].bitcast(I32),
+                in_=w_words[t][PAIR * h : PAIR * (h + 1)].rearrange("g p n -> p g n").bitcast(I32),
+            )
+
+        def load_tail(c):
+            nc.sync.dma_start(
+                out=tail[c][:].bitcast(I32),
+                in_=Wk_words[PASSES - PAIR : PASSES, :, 4 * N_TILE * c : 4 * N_TILE * (c + 1)].rearrange("g p n -> p g n").bitcast(I32),
+            )
 
         def load_scale_rows(plane, rows):
             for r in range(4):
@@ -53,35 +65,32 @@ def tile_mla_pa_kernel(tc, x_words, x_scales, Wq_words, Wq_scales, Wk_words, Wk_
                     in_=rows[:, r:16:4, :].rearrange("g q n -> q g n").bitcast(I32),
                 )
 
-        def load_scales(t):
-            for p in (0, 1, 2, 3, 32, 33, 34, 35):
-                q = 4 * (p // 32) + p % 32
-                nc.sync.dma_start(
-                    out=planes[t][p:P:64, :, :].bitcast(I32),
-                    in_=w_scales[t][:, q:16:8, :].rearrange("g q n -> q g n").bitcast(I32),
-                )
+        def load_scales(t, run):
+            load_scale_rows(planes[t][run], w_scales[t][run * RUN : (run + 1) * RUN])
 
-        def multiply(t, g, accs):
-            for j in range(TILES):
-                nc.tensor.matmul_mx(
-                    out=accs[j][:],
-                    lhsT=xw[:, g, :].bitcast(FP4X4),
-                    lhsT_scale=xs[:, g, :],
-                    rhs=codes[t][g][:, 2 * N_TILE * j : 2 * N_TILE * (j + 1)].bitcast(FP4X4),
-                    rhs_scale=planes[t][:, g, N_TILE * j : N_TILE * (j + 1)],
-                    start=(g == 0),
-                    stop=(g == PASSES - 1),
-                )
+        def multiply(t, g, j, acc):
+            if t == 1 and g >= PASSES - PAIR:
+                rhs = tail[j // 2][:, g - (PASSES - PAIR), 2 * N_TILE * (j % 2) : 2 * N_TILE * (j % 2 + 1)]
+            else:
+                rhs = codes[t][g // PAIR][:, g % PAIR, 2 * N_TILE * j : 2 * N_TILE * (j + 1)]
+            nc.tensor.matmul_mx(
+                out=acc[:],
+                lhsT=xw[:, g, :].bitcast(FP4X4),
+                lhsT_scale=xs[:, g, :],
+                rhs=rhs.bitcast(FP4X4),
+                rhs_scale=planes[t][g // RUN][:, g % RUN, N_TILE * j : N_TILE * (j + 1)],
+                start=(g == 0),
+                stop=(g == PASSES - 1),
+            )
 
         zero(xs[:].rearrange("p g n -> p (g n)"))
-        zero(planes[0][:].rearrange("p g n -> p (g n)"))
+        zero(planes[0][0][:].rearrange("p g n -> p (g n)"))
         nc.sync.dma_start(out=xw[:].bitcast(I32), in_=x_words.rearrange("g p n -> p g n").bitcast(I32))
         load_codes(0, 0)
-        load_codes(0, 1)
         load_scale_rows(xs, x_scales)
-        load_scales(0)
-        for g in range(2, PASSES):
-            load_codes(0, g)
+        load_scales(0, 0)
+        load_codes(0, 1)
+        load_codes(0, 2)
 
         pos_i = keep.tile([P, 1], I32, name="pos_i")
         nc.gpsimd.iota(pos_i[0:64, :], pattern=[[0, 1]], base=0, channel_multiplier=1)
@@ -112,10 +121,16 @@ def tile_mla_pa_kernel(tc, x_words, x_scales, Wq_words, Wq_scales, Wk_words, Wk_
         for h in range(3):
             nc.scalar.activation(out=table[:, :, h, :], in_=minus[:].rearrange("p (a c) -> p a c", a=2), func=ACTF.Sin, scale=-TWO_PI)
 
-        zero(planes[1][:].rearrange("p g n -> p (g n)"))
-        load_scales(1)
-        for g in range(PASSES):
-            load_codes(1, g)
+        for t, run in ((0, 1), (1, 0), (1, 1)):
+            zero(planes[t][run][:].rearrange("p g n -> p (g n)"))
+
+        load_scales(0, 1)
+        load_codes(0, 3)
+        load_scales(1, 0)
+        load_codes(1, 0)
+        load_codes(1, 1)
+        load_scales(1, 1)
+        load_codes(1, 2)
 
         def rotate_products(t, j, acc):
             first = (2 - 8 * j) % 3
@@ -145,30 +160,36 @@ def tile_mla_pa_kernel(tc, x_words, x_scales, Wq_words, Wq_scales, Wk_words, Wk_
                         in_=acc[:].rearrange("p (b c) -> p b c", c=BLOCK)[:, c:8:3, :],
                     )
 
-        def finish(t, accs, after):
-            pending = None
-            for j in range(TILES + 1):
-                if j < TILES:
-                    halves = rotate_products(t, j, accs[j])
-                    copy_plain(t, j, accs[j])
-                if pending is not None:
-                    nc.vector.tensor_add(out=pending[0], in0=pending[0], in1=pending[1])
-                    after(j - 1)
-                pending = halves
+        def finish(t, js, accs):
+            halves = []
+            for j in js:
+                halves.append(rotate_products(t, j, accs[j]))
+                copy_plain(t, j, accs[j])
+            for dst, cross in halves:
+                nc.vector.tensor_add(out=dst, in0=dst, in1=cross)
 
         def store(t, lo, hi):
             nc.sync.dma_start(out=out_rows[t][:, lo:hi], in_=res[t][:, lo:hi])
 
         accs = [psum.tile([P, N_TILE], F32, name="accq%d" % j, tag="acc") for j in range(TILES)]
         for g in range(PASSES):
-            multiply(0, g, accs)
-        finish(0, accs, lambda j: None)
+            for j in range(TILES):
+                multiply(0, g, j, accs[j])
+        for c in range(TILES // 2):
+            finish(0, (2 * c, 2 * c + 1), accs)
 
-        store(0, 0, 1024)
-        store(0, 1024, 2048)
-        store(0, 2048, 3072)
+        store(0, 0, COLS // 2)
+        for c in range(TILES // 2):
+            load_tail(c)
+        store(0, COLS // 2, COLS)
 
         accs = [psum.tile([P, N_TILE], F32, name="acck%d" % j, tag="acc") for j in range(TILES)]
-        for g in range(PASSES):
-            multiply(1, g, accs)
-        finish(1, accs, lambda j: store(1, N_TILE * j, N_TILE * (j + 1)))
+        for g in range(PASSES - PAIR):
+            for j in range(TILES):
+                multiply(1, g, j, accs[j])
+        for c in range(TILES // 2):
+            for j in (2 * c, 2 * c + 1):
+                for g in range(PASSES - PAIR, PASSES):
+                    multiply(1, g, j, accs[j])
+            finish(1, (2 * c, 2 * c + 1), accs)
+            store(1, 2 * N_TILE * c, 2 * N_TILE * (c + 1))

@@ -14,7 +14,6 @@ PASSES = 8
 COLS = 3072
 N_TILE = 512
 TILES = COLS // N_TILE
-RUN = 4
 PAIR = 2
 BLOCK = 64
 PAIRS = 32
@@ -40,11 +39,13 @@ def tile_mla_pa_kernel(tc, x_words, x_scales, Wq_words, Wq_scales, Wk_words, Wk_
         xs = keep.tile([P, PASSES, P], U8, name="xs", align_bytes=64)
         codes = [[keep.tile([P, PAIR, 2 * COLS], U8, name="w%d_%d" % (t, h), align_bytes=64) for h in range(PASSES // PAIR - t)] for t in range(2)]
         tail = [keep.tile([P, PAIR, 4 * N_TILE], U8, name="tail%d" % c, align_bytes=64) for c in range(TILES // 2)]
-        planes = [[keep.tile([P, RUN, COLS], U8, name="s%d_%d" % (t, r), align_bytes=64) for r in range(PASSES // RUN)] for t in range(2)]
+        runs = [((0, 2), (2, 4), (4, 8)), ((0, 4), (4, 8))]
+        planes = [[keep.tile([P, hi - lo, COLS], U8, name="s%d_%d" % (t, lo), align_bytes=64) for lo, hi in runs[t]] for t in range(2)]
         res = [keep.tile([P, COLS], F32, name="res%d" % t) for t in range(2)]
 
         def zero(plane):
-            nc.vector.memset(plane.bitcast(I32), 0)
+            for g in range(plane.shape[1]):
+                nc.vector.memset(plane[:, g, :].bitcast(I32), 0)
 
         def load_codes(t, h):
             nc.sync.dma_start(
@@ -66,7 +67,18 @@ def tile_mla_pa_kernel(tc, x_words, x_scales, Wq_words, Wq_scales, Wk_words, Wk_
                 )
 
         def load_scales(t, run):
-            load_scale_rows(planes[t][run], w_scales[t][run * RUN : (run + 1) * RUN])
+            lo, hi = runs[t][run]
+            for r in range(4):
+                nc.gpsimd.dma_start(
+                    out=planes[t][run][r:P:32, :, :].bitcast(F32),
+                    in_=w_scales[t][lo:hi, r:16:4, :].rearrange("g q n -> q g n").bitcast(F32),
+                )
+
+        def plane_of(t, g):
+            for run, (lo, hi) in enumerate(runs[t]):
+                if lo <= g < hi:
+                    return planes[t][run][:, g - lo, :]
+            return None
 
         def multiply(t, g, j, acc):
             if t == 1 and g >= PASSES - PAIR:
@@ -78,23 +90,28 @@ def tile_mla_pa_kernel(tc, x_words, x_scales, Wq_words, Wq_scales, Wk_words, Wk_
                 lhsT=xw[:, g, :].bitcast(FP4X4),
                 lhsT_scale=xs[:, g, :],
                 rhs=rhs.bitcast(FP4X4),
-                rhs_scale=planes[t][g // RUN][:, g % RUN, N_TILE * j : N_TILE * (j + 1)],
+                rhs_scale=plane_of(t, g)[:, N_TILE * j : N_TILE * (j + 1)],
                 start=(g == 0),
                 stop=(g == PASSES - 1),
             )
 
-        zero(xs[:].rearrange("p g n -> p (g n)"))
-        zero(planes[0][0][:].rearrange("p g n -> p (g n)"))
+        nc.vector.memset(xs[:].rearrange("p g n -> p (g n)").bitcast(I32), 0)
+        zero(planes[0][0])
+        zero(planes[0][1])
         nc.sync.dma_start(out=xw[:].bitcast(I32), in_=x_words.rearrange("g p n -> p g n").bitcast(I32))
-        load_codes(0, 0)
         load_scale_rows(xs, x_scales)
-        load_scales(0, 0)
-        load_codes(0, 1)
-        load_codes(0, 2)
+        for h in range(4):
+            load_codes(0, h)
+        for h in range(3):
+            load_codes(1, h)
+        for c in range(TILES // 2):
+            load_tail(c)
 
         pos_i = keep.tile([P, 1], I32, name="pos_i")
         nc.gpsimd.iota(pos_i[0:64, :], pattern=[[0, 1]], base=0, channel_multiplier=1)
         nc.gpsimd.iota(pos_i[64:128, :], pattern=[[0, 1]], base=0, channel_multiplier=1)
+        load_scales(0, 0)
+        load_scales(0, 1)
         pos = keep.tile([P, 1], F32, name="pos")
         nc.vector.tensor_copy(out=pos[:], in_=pos_i[:])
         theta = keep.tile([P, PAIRS], F32, name="theta")
@@ -120,17 +137,10 @@ def tile_mla_pa_kernel(tc, x_words, x_scales, Wq_words, Wq_scales, Wk_words, Wk_
         table = keep.tile([P, 2, 3, BLOCK], F32, name="table")
         for h in range(3):
             nc.scalar.activation(out=table[:, :, h, :], in_=minus[:].rearrange("p (a c) -> p a c", a=2), func=ACTF.Sin, scale=-TWO_PI)
+        for t, run in ((0, 2), (1, 0), (1, 1)):
+            zero(planes[t][run])
+            load_scales(t, run)
 
-        for t, run in ((0, 1), (1, 0), (1, 1)):
-            zero(planes[t][run][:].rearrange("p g n -> p (g n)"))
-
-        load_scales(0, 1)
-        load_codes(0, 3)
-        load_scales(1, 0)
-        load_codes(1, 0)
-        load_codes(1, 1)
-        load_scales(1, 1)
-        load_codes(1, 2)
 
         def rotate_products(t, j, acc):
             first = (2 - 8 * j) % 3
@@ -171,25 +181,15 @@ def tile_mla_pa_kernel(tc, x_words, x_scales, Wq_words, Wq_scales, Wk_words, Wk_
         def store(t, lo, hi):
             nc.sync.dma_start(out=out_rows[t][:, lo:hi], in_=res[t][:, lo:hi])
 
-        accs = [psum.tile([P, N_TILE], F32, name="accq%d" % j, tag="acc") for j in range(TILES)]
-        for g in range(PASSES):
-            for j in range(TILES):
-                multiply(0, g, j, accs[j])
-        for c in range(TILES // 2):
-            finish(0, (2 * c, 2 * c + 1), accs)
-
-        store(0, 0, COLS // 2)
-        for c in range(TILES // 2):
-            load_tail(c)
-        store(0, COLS // 2, COLS)
-
-        accs = [psum.tile([P, N_TILE], F32, name="acck%d" % j, tag="acc") for j in range(TILES)]
-        for g in range(PASSES - PAIR):
-            for j in range(TILES):
-                multiply(1, g, j, accs[j])
-        for c in range(TILES // 2):
-            for j in (2 * c, 2 * c + 1):
-                for g in range(PASSES - PAIR, PASSES):
-                    multiply(1, g, j, accs[j])
-            finish(1, (2 * c, 2 * c + 1), accs)
-            store(1, 2 * N_TILE * c, 2 * N_TILE * (c + 1))
+        HALF = PASSES // 2
+        for t in range(2):
+            accs = [psum.tile([P, N_TILE], F32, name="acc%d_%d" % (t, j), tag="acc") for j in range(TILES)]
+            for g in range(HALF):
+                for j in range(TILES):
+                    multiply(t, g, j, accs[j])
+            for c in range(TILES // 2):
+                for j in (2 * c, 2 * c + 1):
+                    for g in range(HALF, PASSES):
+                        multiply(t, g, j, accs[j])
+                finish(t, (2 * c, 2 * c + 1), accs)
+                store(t, 2 * N_TILE * c, 2 * N_TILE * (c + 1))

@@ -37,9 +37,9 @@ def tile_mla_pa_kernel(tc, x_words, x_scales, Wq_words, Wq_scales, Wk_words, Wk_
 
         xw = keep.tile([P, PASSES, 256], U8, name="xw", align_bytes=64)
         xs = keep.tile([P, PASSES, P], U8, name="xs", align_bytes=64)
-        codes = [[keep.tile([P, PAIR, 2 * COLS], U8, name="w%d_%d" % (t, h), align_bytes=64) for h in range(PASSES // PAIR - t)] for t in range(2)]
-        tail = [keep.tile([P, PAIR, 4 * N_TILE], U8, name="tail%d" % c, align_bytes=64) for c in range(TILES // 2)]
-        runs = [((0, 2), (2, 4), (4, 8)), ((0, 4), (4, 8))]
+        codes = [[keep.tile([P, PAIR, 2 * COLS], U8, name="w%d_%d" % (t, h), align_bytes=64) for h in range(PASSES // PAIR - 1)] for t in range(2)]
+        tail = [[keep.tile([P, PAIR, 4 * N_TILE], U8, name="tail%d_%d" % (t, c), align_bytes=64) for c in range(TILES // 2)] for t in range(2)]
+        runs = [((0, 2), (2, 8)), ((0, 8),)]
         planes = [[keep.tile([P, hi - lo, COLS], U8, name="s%d_%d" % (t, lo), align_bytes=64) for lo, hi in runs[t]] for t in range(2)]
         res = [keep.tile([P, COLS], F32, name="res%d" % t) for t in range(2)]
 
@@ -53,10 +53,10 @@ def tile_mla_pa_kernel(tc, x_words, x_scales, Wq_words, Wq_scales, Wk_words, Wk_
                 in_=w_words[t][PAIR * h : PAIR * (h + 1)].rearrange("g p n -> p g n").bitcast(I32),
             )
 
-        def load_tail(c):
+        def load_tail(t, c):
             nc.sync.dma_start(
-                out=tail[c][:].bitcast(I32),
-                in_=Wk_words[PASSES - PAIR : PASSES, :, 4 * N_TILE * c : 4 * N_TILE * (c + 1)].rearrange("g p n -> p g n").bitcast(I32),
+                out=tail[t][c][:].bitcast(I32),
+                in_=w_words[t][PASSES - PAIR : PASSES, :, 4 * N_TILE * c : 4 * N_TILE * (c + 1)].rearrange("g p n -> p g n").bitcast(I32),
             )
 
         def load_scale_rows(plane, rows):
@@ -68,11 +68,7 @@ def tile_mla_pa_kernel(tc, x_words, x_scales, Wq_words, Wq_scales, Wk_words, Wk_
 
         def load_scales(t, run):
             lo, hi = runs[t][run]
-            for r in range(4):
-                nc.gpsimd.dma_start(
-                    out=planes[t][run][r:P:32, :, :].bitcast(F32),
-                    in_=w_scales[t][lo:hi, r:16:4, :].rearrange("g q n -> q g n").bitcast(F32),
-                )
+            load_scale_rows(planes[t][run], w_scales[t][lo:hi])
 
         def plane_of(t, g):
             for run, (lo, hi) in enumerate(runs[t]):
@@ -81,8 +77,8 @@ def tile_mla_pa_kernel(tc, x_words, x_scales, Wq_words, Wq_scales, Wk_words, Wk_
             return None
 
         def multiply(t, g, j, acc):
-            if t == 1 and g >= PASSES - PAIR:
-                rhs = tail[j // 2][:, g - (PASSES - PAIR), 2 * N_TILE * (j % 2) : 2 * N_TILE * (j % 2 + 1)]
+            if g >= PASSES - PAIR:
+                rhs = tail[t][j // 2][:, g - (PASSES - PAIR), 2 * N_TILE * (j % 2) : 2 * N_TILE * (j % 2 + 1)]
             else:
                 rhs = codes[t][g // PAIR][:, g % PAIR, 2 * N_TILE * j : 2 * N_TILE * (j + 1)]
             nc.tensor.matmul_mx(
@@ -95,23 +91,25 @@ def tile_mla_pa_kernel(tc, x_words, x_scales, Wq_words, Wq_scales, Wk_words, Wk_
                 stop=(g == PASSES - 1),
             )
 
-        nc.vector.memset(xs[:].rearrange("p g n -> p (g n)").bitcast(I32), 0)
-        zero(planes[0][0])
-        zero(planes[0][1])
-        nc.sync.dma_start(out=xw[:].bitcast(I32), in_=x_words.rearrange("g p n -> p g n").bitcast(I32))
-        load_scale_rows(xs, x_scales)
-        for h in range(4):
-            load_codes(0, h)
-        for h in range(3):
-            load_codes(1, h)
-        for c in range(TILES // 2):
-            load_tail(c)
-
         pos_i = keep.tile([P, 1], I32, name="pos_i")
         nc.gpsimd.iota(pos_i[0:64, :], pattern=[[0, 1]], base=0, channel_multiplier=1)
         nc.gpsimd.iota(pos_i[64:128, :], pattern=[[0, 1]], base=0, channel_multiplier=1)
-        load_scales(0, 0)
-        load_scales(0, 1)
+        nc.vector.memset(xs[:].rearrange("p g n -> p (g n)").bitcast(I32), 0)
+        for t in range(2):
+            for plane in planes[t]:
+                zero(plane)
+        nc.sync.dma_start(out=xw[:].bitcast(I32), in_=x_words.rearrange("g p n -> p g n").bitcast(I32))
+        load_scale_rows(xs, x_scales)
+        for t in range(2):
+            for run in range(len(runs[t])):
+                load_scales(t, run)
+        nc.gpsimd.tensor_copy(out=codes[0][0][0:3, 0, 0:4].bitcast(I32), in_=planes[1][0][0:3, 0, 0:4].bitcast(I32))
+        for t in range(2):
+            for h in range(PASSES // PAIR - 1):
+                load_codes(t, h)
+            for c in range(TILES // 2):
+                load_tail(t, c)
+
         pos = keep.tile([P, 1], F32, name="pos")
         nc.vector.tensor_copy(out=pos[:], in_=pos_i[:])
         theta = keep.tile([P, PAIRS], F32, name="theta")
@@ -137,9 +135,6 @@ def tile_mla_pa_kernel(tc, x_words, x_scales, Wq_words, Wq_scales, Wk_words, Wk_
         table = keep.tile([P, 2, 3, BLOCK], F32, name="table")
         for h in range(3):
             nc.scalar.activation(out=table[:, :, h, :], in_=minus[:].rearrange("p (a c) -> p a c", a=2), func=ACTF.Sin, scale=-TWO_PI)
-        for t, run in ((0, 2), (1, 0), (1, 1)):
-            zero(planes[t][run])
-            load_scales(t, run)
 
 
         def rotate_products(t, j, acc):
@@ -181,15 +176,14 @@ def tile_mla_pa_kernel(tc, x_words, x_scales, Wq_words, Wq_scales, Wk_words, Wk_
         def store(t, lo, hi):
             nc.sync.dma_start(out=out_rows[t][:, lo:hi], in_=res[t][:, lo:hi])
 
-        HALF = PASSES // 2
         for t in range(2):
             accs = [psum.tile([P, N_TILE], F32, name="acc%d_%d" % (t, j), tag="acc") for j in range(TILES)]
-            for g in range(HALF):
+            for g in range(PASSES - PAIR):
                 for j in range(TILES):
                     multiply(t, g, j, accs[j])
             for c in range(TILES // 2):
                 for j in (2 * c, 2 * c + 1):
-                    for g in range(HALF, PASSES):
+                    for g in range(PASSES - PAIR, PASSES):
                         multiply(t, g, j, accs[j])
                 finish(t, (2 * c, 2 * c + 1), accs)
                 store(t, 2 * N_TILE * c, 2 * N_TILE * (c + 1))

@@ -15,6 +15,7 @@ COLS = 3072
 N_TILE = 512
 TILES = COLS // N_TILE
 PAIR = 2
+FRONT = 4
 BLOCK = 64
 PAIRS = 32
 TWO_PI = 6.283185307179586
@@ -37,21 +38,17 @@ def tile_mla_pa_kernel(tc, x_words, x_scales, Wq_words, Wq_scales, Wk_words, Wk_
 
         xw = keep.tile([P, PASSES, 256], U8, name="xw", align_bytes=64)
         xs = keep.tile([P, PASSES, P], U8, name="xs", align_bytes=64)
-        codes = [[keep.tile([P, PAIR, 2 * COLS], U8, name="w%d_%d" % (t, h), align_bytes=64) for h in range(PASSES // PAIR - 1)] for t in range(2)]
+        codes = [[keep.tile([P, 2 * COLS], U8, name="w%d_%d" % (t, g), align_bytes=64) for g in range(PASSES - PAIR)] for t in range(2)]
         tail = [[keep.tile([P, PAIR, 4 * N_TILE], U8, name="tail%d_%d" % (t, c), align_bytes=64) for c in range(TILES // 2)] for t in range(2)]
-        runs = [((0, 2), (2, 8)), ((0, 8),)]
+        runs = [((0, 8),), ((0, 8),)]
         planes = [[keep.tile([P, hi - lo, COLS], U8, name="s%d_%d" % (t, lo), align_bytes=64) for lo, hi in runs[t]] for t in range(2)]
         res = [keep.tile([P, COLS], F32, name="res%d" % t) for t in range(2)]
 
         def zero(plane):
-            for g in range(plane.shape[1]):
-                nc.vector.memset(plane[:, g, :].bitcast(I32), 0)
+            nc.vector.memset(plane[:].rearrange("p g n -> p (g n)").bitcast(I32), 0)
 
-        def load_codes(t, h):
-            nc.sync.dma_start(
-                out=codes[t][h][:].bitcast(I32),
-                in_=w_words[t][PAIR * h : PAIR * (h + 1)].rearrange("g p n -> p g n").bitcast(I32),
-            )
+        def load_codes(t, g):
+            nc.sync.dma_start(out=codes[t][g][:].bitcast(I32), in_=w_words[t][g].bitcast(I32))
 
         def load_tail(t, c):
             nc.sync.dma_start(
@@ -80,7 +77,7 @@ def tile_mla_pa_kernel(tc, x_words, x_scales, Wq_words, Wq_scales, Wk_words, Wk_
             if g >= PASSES - PAIR:
                 rhs = tail[t][j // 2][:, g - (PASSES - PAIR), 2 * N_TILE * (j % 2) : 2 * N_TILE * (j % 2 + 1)]
             else:
-                rhs = codes[t][g // PAIR][:, g % PAIR, 2 * N_TILE * j : 2 * N_TILE * (j + 1)]
+                rhs = codes[t][g][:, 2 * N_TILE * j : 2 * N_TILE * (j + 1)]
             nc.tensor.matmul_mx(
                 out=acc[:],
                 lhsT=xw[:, g, :].bitcast(FP4X4),
@@ -99,14 +96,16 @@ def tile_mla_pa_kernel(tc, x_words, x_scales, Wq_words, Wq_scales, Wk_words, Wk_
             for plane in planes[t]:
                 zero(plane)
         nc.sync.dma_start(out=xw[:].bitcast(I32), in_=x_words.rearrange("g p n -> p g n").bitcast(I32))
+        for g in range(FRONT):
+            load_codes(0, g)
         load_scale_rows(xs, x_scales)
         for t in range(2):
             for run in range(len(runs[t])):
                 load_scales(t, run)
-        nc.gpsimd.tensor_copy(out=codes[0][0][0:3, 0, 0:4].bitcast(I32), in_=planes[1][0][0:3, 0, 0:4].bitcast(I32))
+        nc.gpsimd.tensor_copy(out=codes[0][FRONT][0:3, 0:4].bitcast(I32), in_=planes[1][0][0:3, 0, 0:4].bitcast(I32))
         for t in range(2):
-            for h in range(PASSES // PAIR - 1):
-                load_codes(t, h)
+            for g in range(FRONT if t == 0 else 0, PASSES - PAIR):
+                load_codes(t, g)
             for c in range(TILES // 2):
                 load_tail(t, c)
 

@@ -15,7 +15,7 @@ COLS = 3072
 N_TILE = 512
 TILES = COLS // N_TILE
 PAIR = 2
-FRONT = 4
+FRONT = 3
 BLOCK = 64
 PAIRS = 32
 TWO_PI = 6.283185307179586
@@ -65,7 +65,11 @@ def tile_mla_pa_kernel(tc, x_words, x_scales, Wq_words, Wq_scales, Wk_words, Wk_
 
         def load_scales(t, run):
             lo, hi = runs[t][run]
-            load_scale_rows(planes[t][run], w_scales[t][lo:hi])
+            for r in range(4):
+                nc.gpsimd.dma_start(
+                    out=planes[t][run][r:P:32, :, :].bitcast(F32),
+                    in_=w_scales[t][lo:hi, r:16:4, :].rearrange("g q n -> q g n").bitcast(F32),
+                )
 
         def plane_of(t, g):
             for run, (lo, hi) in enumerate(runs[t]):
@@ -102,6 +106,7 @@ def tile_mla_pa_kernel(tc, x_words, x_scales, Wq_words, Wq_scales, Wk_words, Wk_
         for t in range(2):
             for run in range(len(runs[t])):
                 load_scales(t, run)
+        nc.gpsimd.tensor_copy(out=codes[0][FRONT][0:4, 0:4].bitcast(I32), in_=planes[0][0][0:4, 0, 0:4].bitcast(I32))
         nc.gpsimd.tensor_copy(out=codes[0][FRONT][0:3, 0:4].bitcast(I32), in_=planes[1][0][0:3, 0, 0:4].bitcast(I32))
         for t in range(2):
             for g in range(FRONT if t == 0 else 0, PASSES - PAIR):

@@ -107,7 +107,6 @@ def tile_mla_pa_kernel(tc, x_words, x_scales, Wq_words, Wq_scales, Wk_words, Wk_
             for run in range(len(runs[t])):
                 load_scales(t, run)
         nc.gpsimd.tensor_copy(out=codes[0][FRONT][0:4, 0:4].bitcast(I32), in_=planes[0][0][0:4, 0, 0:4].bitcast(I32))
-        nc.gpsimd.tensor_copy(out=codes[0][FRONT][0:3, 0:4].bitcast(I32), in_=planes[1][0][0:3, 0, 0:4].bitcast(I32))
         for t in range(2):
             for g in range(FRONT if t == 0 else 0, PASSES - PAIR):
                 load_codes(t, g)

@@ -16,6 +16,7 @@ N_TILE = 512
 TILES = COLS // N_TILE
 PAIR = 2
 FRONT = 3
+ALIGN = 256
 BLOCK = 64
 PAIRS = 32
 TWO_PI = 6.283185307179586
@@ -36,13 +37,13 @@ def tile_mla_pa_kernel(tc, x_words, x_scales, Wq_words, Wq_scales, Wk_words, Wk_
         psum = ctx.enter_context(tc.psum_pool(name="psum", bufs=8))
         ctx.enter_context(tc.manual_schedule())
 
-        xw = keep.tile([P, PASSES, 256], U8, name="xw", align_bytes=64)
-        xs = keep.tile([P, PASSES, P], U8, name="xs", align_bytes=64)
-        codes = [[keep.tile([P, 2 * COLS], U8, name="w%d_%d" % (t, g), align_bytes=64) for g in range(PASSES - PAIR)] for t in range(2)]
-        tail = [[keep.tile([P, PAIR, 4 * N_TILE], U8, name="tail%d_%d" % (t, c), align_bytes=64) for c in range(TILES // 2)] for t in range(2)]
+        xw = keep.tile([P, PASSES, 256], U8, name="xw", align_bytes=ALIGN)
+        xs = keep.tile([P, PASSES, P], U8, name="xs", align_bytes=ALIGN)
+        codes = [[keep.tile([P, 2 * COLS], U8, name="w%d_%d" % (t, g), align_bytes=ALIGN) for g in range(PASSES - PAIR)] for t in range(2)]
+        tail = [[keep.tile([P, PAIR, 4 * N_TILE], U8, name="tail%d_%d" % (t, c), align_bytes=ALIGN) for c in range(TILES // 2)] for t in range(2)]
         runs = [((0, 8),), ((0, 8),)]
-        planes = [[keep.tile([P, hi - lo, COLS], U8, name="s%d_%d" % (t, lo), align_bytes=64) for lo, hi in runs[t]] for t in range(2)]
-        res = [keep.tile([P, COLS], F32, name="res%d" % t) for t in range(2)]
+        planes = [[keep.tile([P, hi - lo, COLS], U8, name="s%d_%d" % (t, lo), align_bytes=ALIGN) for lo, hi in runs[t]] for t in range(2)]
+        res = [keep.tile([P, COLS], F32, name="res%d" % t, align_bytes=ALIGN) for t in range(2)]
 
         def zero(plane):
             nc.vector.memset(plane[:].rearrange("p g n -> p (g n)").bitcast(I32), 0)

@@ -15,7 +15,7 @@ COLS = 3072
 N_TILE = 512
 TILES = COLS // N_TILE
 PAIR = 2
-FRONT = 3
+FRONT = 5
 ALIGN = 256
 BLOCK = 64
 PAIRS = 32

@@ -67,10 +67,11 @@ def tile_mla_pa_kernel(tc, x_words, x_scales, Wq_words, Wq_scales, Wk_words, Wk_
         def load_scales(t, run):
             lo, hi = runs[t][run]
             for r in range(4):
-                nc.gpsimd.dma_start(
-                    out=planes[t][run][r:P:32, :, :].bitcast(F32),
-                    in_=w_scales[t][lo:hi, r:16:4, :].rearrange("g q n -> q g n").bitcast(F32),
-                )
+                for quarter in (0, 2, 1, 3):
+                    nc.sync.dma_start(
+                        out=planes[t][run][32 * quarter + r : 32 * quarter + r + 1, :, :].bitcast(I32),
+                        in_=w_scales[t][lo:hi, 4 * quarter + r : 4 * quarter + r + 1, :].rearrange("g q n -> q g n").bitcast(I32),
+                    )
 
         def plane_of(t, g):
             for run, (lo, hi) in enumerate(runs[t]):
@@ -107,7 +108,6 @@ def tile_mla_pa_kernel(tc, x_words, x_scales, Wq_words, Wq_scales, Wk_words, Wk_
         for t in range(2):
             for run in range(len(runs[t])):
                 load_scales(t, run)
-        nc.gpsimd.tensor_copy(out=codes[0][FRONT][0:4, 0:4].bitcast(I32), in_=planes[0][0][0:4, 0, 0:4].bitcast(I32))
         for t in range(2):
             for g in range(FRONT if t == 0 else 0, PASSES - PAIR):
                 load_codes(t, g)

@@ -39,7 +39,8 @@ def tile_mla_pa_kernel(tc, x_words, x_scales, Wq_words, Wq_scales, Wk_words, Wk_
 
         xw = keep.tile([P, PASSES, 256], U8, name="xw", align_bytes=ALIGN)
         xs = keep.tile([P, PASSES, P], U8, name="xs", align_bytes=ALIGN)
-        codes = [[keep.tile([P, 2 * COLS], U8, name="w%d_%d" % (t, g), align_bytes=ALIGN) for g in range(PASSES - PAIR)] for t in range(2)]
+        front = keep.tile([P, FRONT, 2 * COLS], U8, name="front", align_bytes=ALIGN)
+        codes = [[keep.tile([P, 2 * COLS], U8, name="w%d_%d" % (t, g), align_bytes=ALIGN) for g in range(FRONT if t == 0 else 0, PASSES - PAIR)] for t in range(2)]
         tail = [[keep.tile([P, PAIR, 4 * N_TILE], U8, name="tail%d_%d" % (t, c), align_bytes=ALIGN) for c in range(TILES // 2)] for t in range(2)]
         runs = [((0, 8),), ((0, 8),)]
         planes = [[keep.tile([P, hi - lo, COLS], U8, name="s%d_%d" % (t, lo), align_bytes=ALIGN) for lo, hi in runs[t]] for t in range(2)]
@@ -49,7 +50,7 @@ def tile_mla_pa_kernel(tc, x_words, x_scales, Wq_words, Wq_scales, Wk_words, Wk_
             nc.vector.memset(plane[:].rearrange("p g n -> p (g n)").bitcast(I32), 0)
 
         def load_codes(t, g):
-            nc.sync.dma_start(out=codes[t][g][:].bitcast(I32), in_=w_words[t][g].bitcast(I32))
+            nc.sync.dma_start(out=codes[t][g - (FRONT if t == 0 else 0)][:].bitcast(I32), in_=w_words[t][g].bitcast(I32))
 
         def load_tail(t, c):
             nc.sync.dma_start(
@@ -82,8 +83,10 @@ def tile_mla_pa_kernel(tc, x_words, x_scales, Wq_words, Wq_scales, Wk_words, Wk_
         def multiply(t, g, j, acc):
             if g >= PASSES - PAIR:
                 rhs = tail[t][j // 2][:, g - (PASSES - PAIR), 2 * N_TILE * (j % 2) : 2 * N_TILE * (j % 2 + 1)]
+            elif t == 0 and g < FRONT:
+                rhs = front[:, g, 2 * N_TILE * j : 2 * N_TILE * (j + 1)]
             else:
-                rhs = codes[t][g][:, 2 * N_TILE * j : 2 * N_TILE * (j + 1)]
+                rhs = codes[t][g - (FRONT if t == 0 else 0)][:, 2 * N_TILE * j : 2 * N_TILE * (j + 1)]
             nc.tensor.matmul_mx(
                 out=acc[:],
                 lhsT=xw[:, g, :].bitcast(FP4X4),
@@ -102,8 +105,7 @@ def tile_mla_pa_kernel(tc, x_words, x_scales, Wq_words, Wq_scales, Wk_words, Wk_
             for plane in planes[t]:
                 zero(plane)
         nc.sync.dma_start(out=xw[:].bitcast(I32), in_=x_words.rearrange("g p n -> p g n").bitcast(I32))
-        for g in range(FRONT):
-            load_codes(0, g)
+        nc.sync.dma_start(out=front[:].bitcast(I32), in_=w_words[0][0:FRONT].rearrange("g p n -> p g n").bitcast(I32))
         load_scale_rows(xs, x_scales)
         for t in range(2):
             for run in range(len(runs[t])):
@@ -190,4 +192,7 @@ def tile_mla_pa_kernel(tc, x_words, x_scales, Wq_words, Wq_scales, Wk_words, Wk_
                     for g in range(PASSES - PAIR, PASSES):
                         multiply(t, g, j, accs[j])
                 finish(t, (2 * c, 2 * c + 1), accs)
-                store(t, 2 * N_TILE * c, 2 * N_TILE * (c + 1))
+                if t == 1:
+                    store(t, 2 * N_TILE * c, 2 * N_TILE * (c + 1))
+            if t == 0:
+                store(t, 0, COLS)

@@ -105,8 +105,8 @@ def tile_mla_pa_kernel(tc, x_words, x_scales, Wq_words, Wq_scales, Wk_words, Wk_
             for plane in planes[t]:
                 zero(plane)
         nc.sync.dma_start(out=xw[:].bitcast(I32), in_=x_words.rearrange("g p n -> p g n").bitcast(I32))
-        nc.sync.dma_start(out=front[:].bitcast(I32), in_=w_words[0][0:FRONT].rearrange("g p n -> p g n").bitcast(I32))
         load_scale_rows(xs, x_scales)
+        nc.sync.dma_start(out=front[:].bitcast(I32), in_=w_words[0][0:FRONT].rearrange("g p n -> p g n").bitcast(I32))
         for t in range(2):
             for run in range(len(runs[t])):
                 load_scales(t, run)

from contextlib import ExitStack

import concourse.mybir as mybir

F32 = mybir.dt.float32
I32 = mybir.dt.int32
U8 = mybir.dt.uint8
FP4X4 = mybir.dt.float4_e2m1fn_x4
ALU = mybir.AluOpType
ACTF = mybir.ActivationFunctionType

P = 128
PASSES = 8
COLS = 3072
N_TILE = 512
TILES = COLS // N_TILE
PAIR = 2
FRONT = 5
ALIGN = 256
BLOCK = 64
PAIRS = 32
TWO_PI = 6.283185307179586
ROPE_BASE = 10000.0

FLOPS = 2 * 128 * 4096 * 6144


def tile_mla_pa_kernel(tc, x_words, x_scales, Wq_words, Wq_scales, Wk_words, Wk_scales, out_0, out_1):
    nc = tc.nc
    w_words = [Wq_words, Wk_words]
    w_scales = [Wq_scales, Wk_scales]
    out_rows = [o.rearrange("b s h d -> (b s) (h d)") for o in (out_0, out_1)]

    with ExitStack() as ctx:
        keep = ctx.enter_context(tc.tile_pool(name="keep", bufs=1))
        work = ctx.enter_context(tc.tile_pool(name="work", bufs=4))
        psum = ctx.enter_context(tc.psum_pool(name="psum", bufs=8))
        ctx.enter_context(tc.manual_schedule())

        xw = keep.tile([P, PASSES, 256], U8, name="xw", align_bytes=ALIGN)
        xs = keep.tile([P, PASSES, P], U8, name="xs", align_bytes=ALIGN)
        front = keep.tile([P, FRONT, 2 * COLS], U8, name="front", align_bytes=ALIGN)
        codes = [[keep.tile([P, 2 * COLS], U8, name="w%d_%d" % (t, g), align_bytes=ALIGN) for g in range(FRONT if t == 0 else 0, PASSES - PAIR)] for t in range(2)]
        tail = [[keep.tile([P, PAIR, 4 * N_TILE], U8, name="tail%d_%d" % (t, c), align_bytes=ALIGN) for c in range(TILES // 2)] for t in range(2)]
        runs = [((0, 8),), ((0, 8),)]
        planes = [[keep.tile([P, hi - lo, COLS], U8, name="s%d_%d" % (t, lo), align_bytes=ALIGN) for lo, hi in runs[t]] for t in range(2)]
        res = [keep.tile([P, COLS], F32, name="res%d" % t, align_bytes=ALIGN) for t in range(2)]

        def zero(plane):
            nc.vector.memset(plane[:].rearrange("p g n -> p (g n)").bitcast(I32), 0)

        def load_codes(t, g):
            nc.sync.dma_start(out=codes[t][g - (FRONT if t == 0 else 0)][:].bitcast(I32), in_=w_words[t][g].bitcast(I32))

        def load_tail(t, c):
            nc.sync.dma_start(
                out=tail[t][c][:].bitcast(I32),
                in_=w_words[t][PASSES - PAIR : PASSES, :, 4 * N_TILE * c : 4 * N_TILE * (c + 1)].rearrange("g p n -> p g n").bitcast(I32),
            )

        def load_scale_rows(plane, rows):
            for r in range(4):
                nc.sync.dma_start(
                    out=plane[r:P:32, :, :].bitcast(I32),
                    in_=rows[:, r:16:4, :].rearrange("g q n -> q g n").bitcast(I32),
                )

        def load_scales(t, run):
            lo, hi = runs[t][run]
            for r in range(4):
                for quarter in (0, 2, 1, 3):
                    nc.sync.dma_start(
                        out=planes[t][run][32 * quarter + r : 32 * quarter + r + 1, :, :].bitcast(I32),
                        in_=w_scales[t][lo:hi, 4 * quarter + r : 4 * quarter + r + 1, :].rearrange("g q n -> q g n").bitcast(I32),
                    )

        def plane_of(t, g):
            for run, (lo, hi) in enumerate(runs[t]):
                if lo <= g < hi:
                    return planes[t][run][:, g - lo, :]
            return None

        def multiply(t, g, j, acc):
            if g >= PASSES - PAIR:
                rhs = tail[t][j // 2][:, g - (PASSES - PAIR), 2 * N_TILE * (j % 2) : 2 * N_TILE * (j % 2 + 1)]
            elif t == 0 and g < FRONT:
                rhs = front[:, g, 2 * N_TILE * j : 2 * N_TILE * (j + 1)]
            else:
                rhs = codes[t][g - (FRONT if t == 0 else 0)][:, 2 * N_TILE * j : 2 * N_TILE * (j + 1)]
            nc.tensor.matmul_mx(
                out=acc[:],
                lhsT=xw[:, g, :].bitcast(FP4X4),
                lhsT_scale=xs[:, g, :],
                rhs=rhs.bitcast(FP4X4),
                rhs_scale=plane_of(t, g)[:, N_TILE * j : N_TILE * (j + 1)],
                start=(g == 0),
                stop=(g == PASSES - 1),
            )

        pos_i = keep.tile([P, 1], I32, name="pos_i")
        nc.gpsimd.iota(pos_i[0:64, :], pattern=[[0, 1]], base=0, channel_multiplier=1)
        nc.gpsimd.iota(pos_i[64:128, :], pattern=[[0, 1]], base=0, channel_multiplier=1)
        nc.vector.memset(xs[:].rearrange("p g n -> p (g n)").bitcast(I32), 0)
        for t in range(2):
            for plane in planes[t]:
                zero(plane)
        nc.sync.dma_start(out=xw[:].bitcast(I32), in_=x_words.rearrange("g p n -> p g n").bitcast(I32))
        load_scale_rows(xs, x_scales)
        nc.sync.dma_start(out=front[:].bitcast(I32), in_=w_words[0][0:FRONT].rearrange("g p n -> p g n").bitcast(I32))
        for t in range(2):
            for run in range(len(runs[t])):
                load_scales(t, run)
        for t in range(2):
            for g in range(FRONT if t == 0 else 0, PASSES - PAIR):
                load_codes(t, g)
            for c in range(TILES // 2):
                load_tail(t, c)

        pos = keep.tile([P, 1], F32, name="pos")
        nc.vector.tensor_copy(out=pos[:], in_=pos_i[:])
        theta = keep.tile([P, PAIRS], F32, name="theta")
        nc.vector.memset(theta[:, 0:1], 1.0)
        width = 1
        while width < PAIRS:
            nc.vector.tensor_scalar_mul(out=theta[:, width : 2 * width], in0=theta[:, 0:width], scalar1=ROPE_BASE ** (-2.0 * width / BLOCK))
            width *= 2
        turns = keep.tile([P, PAIRS], F32, name="turns")
        nc.vector.tensor_scalar(out=turns[:], in0=theta[:], scalar1=pos[:, 0:1], scalar2=1.0 / TWO_PI, op0=ALU.mult, op1=ALU.mult)
        phase = keep.tile([P, 2, PAIRS, 2], F32, name="phase")
        for a, t, shift in ((0, 0, 0.25), (0, 1, 0.25), (1, 0, 0.5), (1, 1, 0.0)):
            nc.vector.tensor_scalar_add(out=phase[:, a, :, t], in0=turns[:], scalar1=shift)
        flat = phase[:].rearrange("p a i t -> p (a i t)")
        whole_i = keep.tile([P, 2 * BLOCK], I32, name="whole_i")
        nc.vector.tensor_copy(out=whole_i[:], in_=flat)
        whole = keep.tile([P, 2 * BLOCK], F32, name="whole")
        nc.vector.tensor_copy(out=whole[:], in_=whole_i[:])
        frac = keep.tile([P, 2 * BLOCK], F32, name="frac")
        nc.vector.tensor_sub(out=frac[:], in0=flat, in1=whole[:])
        minus = keep.tile([P, 2 * BLOCK], F32, name="minus")
        nc.vector.scalar_tensor_tensor(out=minus[:], in0=frac[:], scalar=0.5, in1=frac[:], op0=ALU.is_gt, op1=ALU.subtract)
        table = keep.tile([P, 2, 3, BLOCK], F32, name="table")
        for h in range(3):
            nc.scalar.activation(out=table[:, :, h, :], in_=minus[:].rearrange("p (a c) -> p a c", a=2), func=ACTF.Sin, scale=-TWO_PI)


        def rotate_products(t, j, acc):
            first = (2 - 8 * j) % 3
            count = len(range(first, 8, 3))
            dst = res[t][:, N_TILE * j : N_TILE * (j + 1)].rearrange("p (b c) -> p b c", c=BLOCK)[:, first:8:3, :]
            nc.vector.tensor_tensor(
                out=dst,
                in0=acc[:].rearrange("p (b c) -> p b c", c=BLOCK)[:, first:8:3, :],
                in1=table[:, 0, 0:count, :],
                op=ALU.mult,
            )
            cross = work.tile([P, 3, BLOCK], F32, name="cross", tag="cross")
            nc.vector.tensor_tensor(
                out=cross[:, 0:count, :].rearrange("p b (i t) -> p b i t", t=2),
                in0=acc[:].rearrange("p (b i t) -> p b i t", i=PAIRS, t=2)[:, first:8:3, :, ::-1],
                in1=table[:, 1, 0:count, :].rearrange("p b (i t) -> p b i t", t=2),
                op=ALU.mult,
            )
            return dst, cross[:, 0:count, :]

        def copy_plain(t, j, acc):
            first = (2 - 8 * j) % 3
            for c in range(3):
                if c != first:
                    nc.scalar.copy(
                        out=res[t][:, N_TILE * j : N_TILE * (j + 1)].rearrange("p (b c) -> p b c", c=BLOCK)[:, c:8:3, :],
                        in_=acc[:].rearrange("p (b c) -> p b c", c=BLOCK)[:, c:8:3, :],
                    )

        def finish(t, js, accs):
            halves = []
            for j in js:
                halves.append(rotate_products(t, j, accs[j]))
                copy_plain(t, j, accs[j])
            for dst, cross in halves:
                nc.vector.tensor_add(out=dst, in0=dst, in1=cross)

        def store(t, lo, hi):
            nc.sync.dma_start(out=out_rows[t][:, lo:hi], in_=res[t][:, lo:hi])

        for t in range(2):
            accs = [psum.tile([P, N_TILE], F32, name="acc%d_%d" % (t, j), tag="acc") for j in range(TILES)]
            for g in range(PASSES - PAIR):
                for j in range(TILES):
                    multiply(t, g, j, accs[j])
            for c in range(TILES // 2):
                for j in (2 * c, 2 * c + 1):
                    for g in range(PASSES - PAIR, PASSES):
                        multiply(t, g, j, accs[j])
                finish(t, (2 * c, 2 * c + 1), accs)
                if t == 1:
                    store(t, 2 * N_TILE * c, 2 * N_TILE * (c + 1))
            if t == 0:
                store(t, 0, COLS)
